import numpy as np
import ml_dtypes

BF16 = ml_dtypes.bfloat16


def bf(x):
    return np.asarray(x, np.float32).astype(BF16)


def f32(x):
    return np.asarray(x, np.float32)


def f64(x):
    return np.asarray(x).astype(np.float64)


def striped(idx):
    return np.tile(idx.reshape(-1, 16).T, (8, 1))


C, S, N, T, NH, HD = 256, 4096, 512, 512, 2, 128


def setup_inputs():
    return {
        "base": f32(np.random.standard_normal((C, S))),
        "q": bf(np.random.standard_normal((C, N))),
        "k": bf(np.random.standard_normal((C, T))),
        "v": bf(3.0 * np.random.standard_normal((T, C))),
        "attn_bias": f32(0.5 * np.random.standard_normal((T, N))),
        "offs": striped(np.random.permutation(S)[:N]),
    }


def reference(base, q, k, v, attn_bias, offs):
    idx = offs[:16].T.reshape(-1)
    qh = f64(q).reshape(NH, HD, N)
    kh = f64(k).reshape(NH, HD, T)
    vh = f64(v).reshape(T, NH, HD)
    e = np.exp(np.einsum("hdt,hdn->htn", kh, qh) / np.sqrt(HD) + f64(attn_bias)[None])
    num = np.einsum("thd,htn->hdn", vh, e)
    den = e.sum(axis=1, keepdims=True)
    out = f64(base).copy()
    out[:, idx] = (num * (1.0 / den)).reshape(C, N)
    return out

@@ -1,0 +1,86 @@
+import math
+
+import concourse.mybir as mybir
+
+F32 = mybir.dt.float32
+BF16 = mybir.dt.bfloat16
+U16 = mybir.dt.uint16
+MULT = mybir.AluOpType.mult
+ADD = mybir.AluOpType.add
+EXP = mybir.ActivationFunctionType.Exp
+
+P = 128
+HEADS = 2
+KEYS = 512
+QUERIES = 512
+TOKENS = 4096
+KEY_BLOCKS = KEYS // P
+
+FLOPS = 2 * HEADS * 2 * P * KEYS * QUERIES
+
+
+def tile_llamaattention_kernel(tc, base, q, k, v, attn_bias, offs, out):
+    nc = tc.nc
+    with (
+        tc.tile_pool(name="held", bufs=1) as held,
+        tc.tile_pool(name="logit_pool", bufs=4) as logit_pool,
+        tc.tile_pool(name="weight_pool", bufs=2 * KEY_BLOCKS) as weight_pool,
+        tc.tile_pool(name="head_pool", bufs=HEADS) as head_pool,
+        tc.psum_pool(name="score_banks", bufs=4) as score_banks,
+        tc.psum_pool(name="sum_banks", bufs=HEADS) as sum_banks,
+    ):
+        offsets = held.tile([P, QUERIES // 16], U16, name="offsets")
+        nc.sync.dma_start(offsets[:], offs)
+        k_sb = held.tile([P, HEADS, KEYS], BF16, name="k_sb")
+        nc.sync.dma_start(k_sb[:], k.rearrange("(h p) t -> p h t", p=P))
+        q_sb = held.tile([P, HEADS, QUERIES], BF16, name="q_sb")
+        nc.sync.dma_start(q_sb[:], q.rearrange("(h p) j -> p h j", p=P))
+        bias_sb = []
+        for tb in range(KEY_BLOCKS):
+            bias_tb = held.tile([P, QUERIES], F32, name=f"bias{tb}")
+            nc.sync.dma_start(bias_tb[:], attn_bias[tb * P : (tb + 1) * P, :])
+            bias_sb.append(bias_tb)
+        v_sb = held.tile([P, KEY_BLOCKS, HEADS * P], BF16, name="v_sb")
+        nc.sync.dma_start(v_sb[:], v.rearrange("(tb p) c -> p tb c", p=P))
+        windows = []
+        for h in range(HEADS):
+            window = held.tile([P, TOKENS], F32, name=f"window{h}")
+            nc.sync.dma_start(window[:], base[h * P : (h + 1) * P, :])
+            windows.append(window)
+
+        ones = held.tile([P, P], BF16, name="ones")
+        nc.gpsimd.memset(ones[:], 1.0)
+
+        for h in range(HEADS):
+            weights = []
+            for tb in range(KEY_BLOCKS):
+                scores = score_banks.tile([P, QUERIES], F32, name="scores")
+                nc.tensor.matmul(
+                    scores[:], k_sb[:, h, tb * P : (tb + 1) * P], q_sb[:, h, :], start=True, stop=True
+                )
+                logits = logit_pool.tile([P, QUERIES], F32, name="logits")
+                nc.vector.scalar_tensor_tensor(
+                    logits[:], scores[:], 1.0 / math.sqrt(P), bias_sb[tb][:], MULT, ADD
+                )
+                e_tb = weight_pool.tile([P, QUERIES], BF16, name="e_tb")
+                nc.scalar.activation(e_tb[:], logits[:], EXP)
+                weights.append(e_tb)
+
+            num_ps = sum_banks.tile([P, QUERIES], F32, name="num_ps")
+            den_ps = sum_banks.tile([P, QUERIES], F32, name="den_ps")
+            for tb in range(KEY_BLOCKS):
+                first, last = tb == 0, tb == KEY_BLOCKS - 1
+                nc.tensor.matmul(
+                    num_ps[:], v_sb[:, tb, h * P : (h + 1) * P], weights[tb][:], start=first, stop=last
+                )
+            for tb in range(KEY_BLOCKS):
+                first, last = tb == 0, tb == KEY_BLOCKS - 1
+                nc.tensor.matmul(den_ps[:], ones[:], weights[tb][:], start=first, stop=last)
+
+            num_sb = head_pool.tile([P, QUERIES], F32, name="num_sb")
+            nc.scalar.copy(num_sb[:], num_ps[:])
+            inv_den = head_pool.tile([P, QUERIES], F32, name="inv_den")
+            nc.vector.reciprocal(inv_den[:], den_ps[:])
+
+            nc.vector.tensor_tensor(windows[h][:].indirect(offsets[:]), num_sb[:], inv_den[:], MULT)
+            nc.sync.dma_start(out[h * P : (h + 1) * P, :], windows[h][:])

@@ -1,13 +1,14 @@
 import math
 
 import concourse.mybir as mybir
+from concourse.masks import make_identity
 
 F32 = mybir.dt.float32
 BF16 = mybir.dt.bfloat16
 U16 = mybir.dt.uint16
 MULT = mybir.AluOpType.mult
-ADD = mybir.AluOpType.add
 EXP = mybir.ActivationFunctionType.Exp
+ALONG_ROW = mybir.AxisListType.X
 
 P = 128
 HEADS = 2
@@ -15,6 +16,11 @@ KEYS = 512
 QUERIES = 512
 TOKENS = 4096
 KEY_BLOCKS = KEYS // P
+QUERY_BLOCKS = QUERIES // P
+ROOT = math.sqrt(P)
+
+LOGIT_BANKS = 4
+FLIP_BANKS = 2
 
 FLOPS = 2 * HEADS * 2 * P * KEYS * QUERIES
 
@@ -23,18 +29,18 @@ def tile_llamaattention_kernel(tc, base, q, k, v, attn_bias, offs, out):
     nc = tc.nc
     with (
         tc.tile_pool(name="held", bufs=1) as held,
-        tc.tile_pool(name="logit_pool", bufs=4) as logit_pool,
-        tc.tile_pool(name="weight_pool", bufs=2 * KEY_BLOCKS) as weight_pool,
-        tc.tile_pool(name="head_pool", bufs=HEADS) as head_pool,
-        tc.psum_pool(name="score_banks", bufs=4) as score_banks,
-        tc.psum_pool(name="sum_banks", bufs=HEADS) as sum_banks,
+        tc.tile_pool(name="row_stats", bufs=LOGIT_BANKS) as row_stats,
+        tc.tile_pool(name="weight_pool", bufs=3) as weight_pool,
+        tc.psum_pool(name="logit_banks", bufs=LOGIT_BANKS) as logit_banks,
+        tc.psum_pool(name="flip_banks", bufs=FLIP_BANKS) as flip_banks,
+        tc.psum_pool(name="head_banks", bufs=1) as head_banks,
     ):
         offsets = held.tile([P, QUERIES // 16], U16, name="offsets")
         nc.sync.dma_start(offsets[:], offs)
-        k_sb = held.tile([P, HEADS, KEYS], BF16, name="k_sb")
-        nc.sync.dma_start(k_sb[:], k.rearrange("(h p) t -> p h t", p=P))
         q_sb = held.tile([P, HEADS, QUERIES], BF16, name="q_sb")
         nc.sync.dma_start(q_sb[:], q.rearrange("(h p) j -> p h j", p=P))
+        k_sb = held.tile([P, HEADS, KEYS], BF16, name="k_sb")
+        nc.sync.dma_start(k_sb[:], k.rearrange("(h p) t -> p h t", p=P))
         bias_sb = []
         for tb in range(KEY_BLOCKS):
             bias_tb = held.tile([P, QUERIES], F32, name=f"bias{tb}")
@@ -48,39 +54,88 @@ def tile_llamaattention_kernel(tc, base, q, k, v, attn_bias, offs, out):
             nc.sync.dma_start(window[:], base[h * P : (h + 1) * P, :])
             windows.append(window)
 
-        ones = held.tile([P, P], BF16, name="ones")
-        nc.gpsimd.memset(ones[:], 1.0)
+        ident_f32 = held.tile([P, P], F32, name="ident_f32")
+        make_identity(nc, ident_f32[:])
+        ident_bf16 = held.tile([P, P], BF16, name="ident_bf16")
+        make_identity(nc, ident_bf16[:])
 
-        for h in range(HEADS):
-            weights = []
+        bias_up = []
+        for tb in range(KEY_BLOCKS):
+            bias_up_tb = held.tile([P, QUERIES], F32, name=f"bias_up{tb}")
+            nc.vector.tensor_scalar_mul(bias_up_tb[:], bias_sb[tb][:], ROOT)
+            bias_up.append(bias_up_tb)
+
+        blocks = [(h, jb) for h in range(HEADS) for jb in range(QUERY_BLOCKS)]
+        logit_tiles = {}
+        den = [held.tile([P, QUERY_BLOCKS], F32, name=f"den{h}") for h in range(HEADS)]
+        flipped = [held.tile([P, KEY_BLOCKS, QUERIES], BF16, name=f"flipped{h}") for h in range(HEADS)]
+        num_sb = [held.tile([P, QUERIES], F32, name=f"num_sb{h}") for h in range(HEADS)]
+        inv_den_wide = [held.tile([P, QUERIES], F32, name=f"inv_den_wide{h}") for h in range(HEADS)]
+
+        def make_logits(i):
+            h, jb = blocks[i]
+            queries = slice(jb * P, (jb + 1) * P)
+            logits_ps = logit_banks.tile([P, KEYS], F32, name="logits_ps")
+            nc.tensor.matmul(logits_ps[:], q_sb[:, h, queries], k_sb[:, h, :], start=True, stop=False)
             for tb in range(KEY_BLOCKS):
-                scores = score_banks.tile([P, QUERIES], F32, name="scores")
                 nc.tensor.matmul(
-                    scores[:], k_sb[:, h, tb * P : (tb + 1) * P], q_sb[:, h, :], start=True, stop=True
+                    logits_ps[:, tb * P : (tb + 1) * P],
+                    bias_up[tb][:, queries],
+                    ident_f32[:],
+                    is_transpose=True,
+                    start=False,
+                    stop=tb == KEY_BLOCKS - 1,
                 )
-                logits = logit_pool.tile([P, QUERIES], F32, name="logits")
-                nc.vector.scalar_tensor_tensor(
-                    logits[:], scores[:], 1.0 / math.sqrt(P), bias_sb[tb][:], MULT, ADD
-                )
-                e_tb = weight_pool.tile([P, QUERIES], BF16, name="e_tb")
-                nc.scalar.activation(e_tb[:], logits[:], EXP)
-                weights.append(e_tb)
+            logit_tiles[i] = logits_ps
 
-            num_ps = sum_banks.tile([P, QUERIES], F32, name="num_ps")
-            den_ps = sum_banks.tile([P, QUERIES], F32, name="den_ps")
+        def make_weights(i):
+            h, jb = blocks[i]
+            logits_ps = logit_tiles[i]
+            row_max = row_stats.tile([P, 1], F32, name="row_max")
+            nc.vector.reduce_max(row_max[:], logits_ps[:], axis=ALONG_ROW)
+            shift = row_stats.tile([P, 1], F32, name="shift")
+            nc.vector.tensor_scalar_mul(shift[:], row_max[:], -1.0 / ROOT)
+            e_sb = weight_pool.tile([P, KEYS], BF16, name="e_sb")
+            nc.scalar.activation(
+                e_sb[:], logits_ps[:], EXP, bias=shift[:], scale=1.0 / ROOT, accum_out=den[h][:, jb : jb + 1]
+            )
+            flip_ps = flip_banks.tile([P, KEY_BLOCKS, P], BF16, name="flip_ps")
             for tb in range(KEY_BLOCKS):
-                first, last = tb == 0, tb == KEY_BLOCKS - 1
+                nc.tensor.transpose(flip_ps[:, tb, :], e_sb[:, tb * P : (tb + 1) * P], ident_bf16[:])
+            nc.scalar.copy(flipped[h][:, :, jb * P : (jb + 1) * P], flip_ps[:])
+
+        def make_sums(h):
+            inv_den = row_stats.tile([P, QUERY_BLOCKS], F32, name="inv_den")
+            nc.vector.reciprocal(inv_den[:], den[h][:])
+            spread_ps = head_banks.tile([P, QUERIES], F32, name="spread_ps")
+            for jb in range(QUERY_BLOCKS):
+                nc.tensor.transpose(
+                    spread_ps[:, jb * P : (jb + 1) * P], inv_den[:, jb : jb + 1].to_broadcast([P, P]), ident_f32[:]
+                )
+            nc.scalar.copy(inv_den_wide[h][:], spread_ps[:])
+            num_ps = head_banks.tile([P, QUERIES], F32, name="num_ps")
+            for tb in range(KEY_BLOCKS):
                 nc.tensor.matmul(
-                    num_ps[:], v_sb[:, tb, h * P : (h + 1) * P], weights[tb][:], start=first, stop=last
+                    num_ps[:],
+                    v_sb[:, tb, h * P : (h + 1) * P],
+                    flipped[h][:, tb, :],
+                    start=tb == 0,
+                    stop=tb == KEY_BLOCKS - 1,
                 )
-            for tb in range(KEY_BLOCKS):
-                first, last = tb == 0, tb == KEY_BLOCKS - 1
-                nc.tensor.matmul(den_ps[:], ones[:], weights[tb][:], start=first, stop=last)
+            nc.scalar.copy(num_sb[h][:], num_ps[:])
 
-            num_sb = head_pool.tile([P, QUERIES], F32, name="num_sb")
-            nc.scalar.copy(num_sb[:], num_ps[:])
-            inv_den = head_pool.tile([P, QUERIES], F32, name="inv_den")
-            nc.vector.reciprocal(inv_den[:], den_ps[:])
-
-            nc.vector.tensor_tensor(windows[h][:].indirect(offsets[:]), num_sb[:], inv_den[:], MULT)
+        def place(h):
+            nc.vector.tensor_tensor(windows[h][:].indirect(offsets[:]), num_sb[h][:], inv_den_wide[h][:], MULT)
             nc.sync.dma_start(out[h * P : (h + 1) * P, :], windows[h][:])
+
+        for i in range(LOGIT_BANKS):
+            make_logits(i)
+        for i, (h, jb) in enumerate(blocks):
+            make_weights(i)
+            if i + LOGIT_BANKS < len(blocks):
+                make_logits(i + LOGIT_BANKS)
+            if jb == QUERY_BLOCKS - 1:
+                if h > 0:
+                    place(h - 1)
+                make_sums(h)
+        place(HEADS - 1)

@@ -30,22 +30,26 @@ def tile_llamaattention_kernel(tc, base, q, k, v, attn_bias, offs, out):
     with (
         tc.tile_pool(name="held", bufs=1) as held,
         tc.tile_pool(name="row_stats", bufs=LOGIT_BANKS) as row_stats,
-        tc.tile_pool(name="weight_pool", bufs=3) as weight_pool,
+        tc.tile_pool(name="weight_pool", bufs=HEADS * QUERY_BLOCKS) as weight_pool,
         tc.psum_pool(name="logit_banks", bufs=LOGIT_BANKS) as logit_banks,
         tc.psum_pool(name="flip_banks", bufs=FLIP_BANKS) as flip_banks,
         tc.psum_pool(name="head_banks", bufs=1) as head_banks,
     ):
         offsets = held.tile([P, QUERIES // 16], U16, name="offsets")
         nc.sync.dma_start(offsets[:], offs)
-        q_sb = held.tile([P, HEADS, QUERIES], BF16, name="q_sb")
-        nc.sync.dma_start(q_sb[:], q.rearrange("(h p) j -> p h j", p=P))
-        k_sb = held.tile([P, HEADS, KEYS], BF16, name="k_sb")
-        nc.sync.dma_start(k_sb[:], k.rearrange("(h p) t -> p h t", p=P))
+        q_sb = [held.tile([P, QUERIES], BF16, name=f"q_sb{h}") for h in range(HEADS)]
+        k_sb = [held.tile([P, KEYS], BF16, name=f"k_sb{h}") for h in range(HEADS)]
+        nc.sync.dma_start(q_sb[0][:], q[0:P, :])
+        nc.sync.dma_start(k_sb[0][:], k[0:P, :])
+        bias_by_keys = attn_bias.rearrange("(tb p) j -> p tb j", p=P)
         bias_sb = []
-        for tb in range(KEY_BLOCKS):
-            bias_tb = held.tile([P, QUERIES], F32, name=f"bias{tb}")
-            nc.sync.dma_start(bias_tb[:], attn_bias[tb * P : (tb + 1) * P, :])
-            bias_sb.append(bias_tb)
+        for jb in range(QUERY_BLOCKS):
+            bias_jb = held.tile([P, KEY_BLOCKS, P], F32, name=f"bias{jb}")
+            nc.sync.dma_start(bias_jb[:], bias_by_keys[:, :, jb * P : (jb + 1) * P])
+            bias_sb.append(bias_jb)
+        for h in range(1, HEADS):
+            nc.sync.dma_start(q_sb[h][:], q[h * P : (h + 1) * P, :])
+            nc.sync.dma_start(k_sb[h][:], k[h * P : (h + 1) * P, :])
         v_sb = held.tile([P, KEY_BLOCKS, HEADS * P], BF16, name="v_sb")
         nc.sync.dma_start(v_sb[:], v.rearrange("(tb p) c -> p tb c", p=P))
         windows = []
@@ -60,10 +64,13 @@ def tile_llamaattention_kernel(tc, base, q, k, v, attn_bias, offs, out):
         make_identity(nc, ident_bf16[:])
 
         bias_up = []
-        for tb in range(KEY_BLOCKS):
-            bias_up_tb = held.tile([P, QUERIES], F32, name=f"bias_up{tb}")
-            nc.vector.tensor_scalar_mul(bias_up_tb[:], bias_sb[tb][:], ROOT)
-            bias_up.append(bias_up_tb)
+        for jb in range(QUERY_BLOCKS):
+            bias_up_jb = held.tile([P, KEY_BLOCKS, P], F32, name=f"bias_up{jb}")
+            if jb == 0:
+                nc.vector.tensor_scalar_mul(bias_up_jb[:], bias_sb[jb][:], ROOT)
+            else:
+                nc.gpsimd.tensor_scalar(bias_up_jb[:], bias_sb[jb][:], ROOT, 1.0, MULT, MULT)
+            bias_up.append(bias_up_jb)
 
         blocks = [(h, jb) for h in range(HEADS) for jb in range(QUERY_BLOCKS)]
         logit_tiles = {}
@@ -74,18 +81,19 @@ def tile_llamaattention_kernel(tc, base, q, k, v, attn_bias, offs, out):
 
         def make_logits(i):
             h, jb = blocks[i]
-            queries = slice(jb * P, (jb + 1) * P)
             logits_ps = logit_banks.tile([P, KEYS], F32, name="logits_ps")
-            nc.tensor.matmul(logits_ps[:], q_sb[:, h, queries], k_sb[:, h, :], start=True, stop=False)
             for tb in range(KEY_BLOCKS):
                 nc.tensor.matmul(
                     logits_ps[:, tb * P : (tb + 1) * P],
-                    bias_up[tb][:, queries],
+                    bias_up[jb][:, tb, :],
                     ident_f32[:],
                     is_transpose=True,
-                    start=False,
-                    stop=tb == KEY_BLOCKS - 1,
+                    start=tb == 0,
+                    stop=False,
                 )
+            nc.tensor.matmul(
+                logits_ps[:], q_sb[h][:, jb * P : (jb + 1) * P], k_sb[h][:], start=False, stop=True
+            )
             logit_tiles[i] = logits_ps
 
         def make_weights(i):

@@ -35,23 +35,24 @@ def tile_llamaattention_kernel(tc, base, q, k, v, attn_bias, offs, out):
         tc.psum_pool(name="flip_banks", bufs=FLIP_BANKS) as flip_banks,
         tc.psum_pool(name="head_banks", bufs=1) as head_banks,
     ):
-        offsets = held.tile([P, QUERIES // 16], U16, name="offsets")
-        nc.sync.dma_start(offsets[:], offs)
         q_sb = [held.tile([P, QUERIES], BF16, name=f"q_sb{h}") for h in range(HEADS)]
         k_sb = [held.tile([P, KEYS], BF16, name=f"k_sb{h}") for h in range(HEADS)]
-        nc.sync.dma_start(q_sb[0][:], q[0:P, :])
-        nc.sync.dma_start(k_sb[0][:], k[0:P, :])
         bias_by_keys = attn_bias.rearrange("(tb p) j -> p tb j", p=P)
         bias_sb = []
         for jb in range(QUERY_BLOCKS):
             bias_jb = held.tile([P, KEY_BLOCKS, P], F32, name=f"bias{jb}")
             nc.sync.dma_start(bias_jb[:], bias_by_keys[:, :, jb * P : (jb + 1) * P])
             bias_sb.append(bias_jb)
+            if jb == 0:
+                nc.sync.dma_start(q_sb[0][:], q[0:P, :])
+                nc.sync.dma_start(k_sb[0][:], k[0:P, :])
         for h in range(1, HEADS):
             nc.sync.dma_start(q_sb[h][:], q[h * P : (h + 1) * P, :])
             nc.sync.dma_start(k_sb[h][:], k[h * P : (h + 1) * P, :])
         v_sb = held.tile([P, KEY_BLOCKS, HEADS * P], BF16, name="v_sb")
         nc.sync.dma_start(v_sb[:], v.rearrange("(tb p) c -> p tb c", p=P))
+        offsets = held.tile([P, QUERIES // 16], U16, name="offsets")
+        nc.sync.dma_start(offsets[:], offs)
         windows = []
         for h in range(HEADS):
             window = held.tile([P, TOKENS], F32, name=f"window{h}")
@@ -122,14 +123,15 @@ def tile_llamaattention_kernel(tc, base, q, k, v, attn_bias, offs, out):
                 )
             nc.scalar.copy(inv_den_wide[h][:], spread_ps[:])
             num_ps = head_banks.tile([P, QUERIES], F32, name="num_ps")
-            for tb in range(KEY_BLOCKS):
-                nc.tensor.matmul(
-                    num_ps[:],
-                    v_sb[:, tb, h * P : (h + 1) * P],
-                    flipped[h][:, tb, :],
-                    start=tb == 0,
-                    stop=tb == KEY_BLOCKS - 1,
-                )
+            for first, last in ((0, QUERIES - P), (QUERIES - P, QUERIES)):
+                for tb in range(KEY_BLOCKS):
+                    nc.tensor.matmul(
+                        num_ps[:, first:last],
+                        v_sb[:, tb, h * P : (h + 1) * P],
+                        flipped[h][:, tb, first:last],
+                        start=tb == 0,
+                        stop=tb == KEY_BLOCKS - 1,
+                    )
             nc.scalar.copy(num_sb[h][:], num_ps[:])
 
         def place(h):

@@ -111,7 +111,10 @@ def tile_llamaattention_kernel(tc, base, q, k, v, attn_bias, offs, out):
             flip_ps = flip_banks.tile([P, KEY_BLOCKS, P], BF16, name="flip_ps")
             for tb in range(KEY_BLOCKS):
                 nc.tensor.transpose(flip_ps[:, tb, :], e_sb[:, tb * P : (tb + 1) * P], ident_bf16[:])
-            nc.scalar.copy(flipped[h][:, :, jb * P : (jb + 1) * P], flip_ps[:])
+            if h == 0:
+                nc.vector.tensor_copy(flipped[h][:, :, jb * P : (jb + 1) * P], flip_ps[:])
+            else:
+                nc.scalar.copy(flipped[h][:, :, jb * P : (jb + 1) * P], flip_ps[:])
 
         def make_sums(h):
             inv_den = row_stats.tile([P, QUERY_BLOCKS], F32, name="inv_den")

@@ -67,10 +67,7 @@ def tile_llamaattention_kernel(tc, base, q, k, v, attn_bias, offs, out):
         bias_up = []
         for jb in range(QUERY_BLOCKS):
             bias_up_jb = held.tile([P, KEY_BLOCKS, P], F32, name=f"bias_up{jb}")
-            if jb == 0:
-                nc.vector.tensor_scalar_mul(bias_up_jb[:], bias_sb[jb][:], ROOT)
-            else:
-                nc.gpsimd.tensor_scalar(bias_up_jb[:], bias_sb[jb][:], ROOT, 1.0, MULT, MULT)
+            nc.vector.tensor_scalar_mul(bias_up_jb[:], bias_sb[jb][:], ROOT)
             bias_up.append(bias_up_jb)
 
         blocks = [(h, jb) for h in range(HEADS) for jb in range(QUERY_BLOCKS)]
@@ -126,7 +123,11 @@ def tile_llamaattention_kernel(tc, base, q, k, v, attn_bias, offs, out):
                 )
             nc.scalar.copy(inv_den_wide[h][:], spread_ps[:])
             num_ps = head_banks.tile([P, QUERIES], F32, name="num_ps")
-            for first, last in ((0, QUERIES - P), (QUERIES - P, QUERIES)):
+            if h == HEADS - 1:
+                column_groups = ((0, QUERIES - P), (QUERIES - P, QUERIES))
+            else:
+                column_groups = ((0, QUERIES),)
+            for first, last in column_groups:
                 for tb in range(KEY_BLOCKS):
                     nc.tensor.matmul(
                         num_ps[:, first:last],

@@ -67,7 +67,10 @@ def tile_llamaattention_kernel(tc, base, q, k, v, attn_bias, offs, out):
         bias_up = []
         for jb in range(QUERY_BLOCKS):
             bias_up_jb = held.tile([P, KEY_BLOCKS, P], F32, name=f"bias_up{jb}")
-            nc.vector.tensor_scalar_mul(bias_up_jb[:], bias_sb[jb][:], ROOT)
+            if jb == 0:
+                nc.vector.tensor_scalar_mul(bias_up_jb[:], bias_sb[jb][:], ROOT)
+            else:
+                nc.scalar.mul(bias_up_jb[:], bias_sb[jb][:], ROOT)
             bias_up.append(bias_up_jb)
 
         blocks = [(h, jb) for h in range(HEADS) for jb in range(QUERY_BLOCKS)]
@@ -136,7 +139,10 @@ def tile_llamaattention_kernel(tc, base, q, k, v, attn_bias, offs, out):
                         start=tb == 0,
                         stop=tb == KEY_BLOCKS - 1,
                     )
-            nc.scalar.copy(num_sb[h][:], num_ps[:])
+            if h == 0:
+                nc.vector.tensor_copy(num_sb[h][:], num_ps[:])
+            else:
+                nc.scalar.copy(num_sb[h][:], num_ps[:])
 
         def place(h):
             nc.vector.tensor_tensor(windows[h][:].indirect(offsets[:]), num_sb[h][:], inv_den_wide[h][:], MULT)

@@ -37,15 +37,14 @@ def tile_llamaattention_kernel(tc, base, q, k, v, attn_bias, offs, out):
     ):
         q_sb = [held.tile([P, QUERIES], BF16, name=f"q_sb{h}") for h in range(HEADS)]
         k_sb = [held.tile([P, KEYS], BF16, name=f"k_sb{h}") for h in range(HEADS)]
+        for sb, src in ((q_sb[0], q), (k_sb[0], k)):
+            nc.sync.dma_start(sb[:], src[0:P, :])
         bias_by_keys = attn_bias.rearrange("(tb p) j -> p tb j", p=P)
         bias_sb = []
         for jb in range(QUERY_BLOCKS):
             bias_jb = held.tile([P, KEY_BLOCKS, P], F32, name=f"bias{jb}")
             nc.sync.dma_start(bias_jb[:], bias_by_keys[:, :, jb * P : (jb + 1) * P])
             bias_sb.append(bias_jb)
-            if jb == 0:
-                nc.sync.dma_start(q_sb[0][:], q[0:P, :])
-                nc.sync.dma_start(k_sb[0][:], k[0:P, :])
         for h in range(1, HEADS):
             nc.sync.dma_start(q_sb[h][:], q[h * P : (h + 1) * P, :])
             nc.sync.dma_start(k_sb[h][:], k[h * P : (h + 1) * P, :])
@@ -83,18 +82,24 @@ def tile_llamaattention_kernel(tc, base, q, k, v, attn_bias, offs, out):
         def make_logits(i):
             h, jb = blocks[i]
             logits_ps = logit_banks.tile([P, KEYS], F32, name="logits_ps")
+            scores_first = i < 2
+            if scores_first:
+                nc.tensor.matmul(
+                    logits_ps[:], q_sb[h][:, jb * P : (jb + 1) * P], k_sb[h][:], start=True, stop=False
+                )
             for tb in range(KEY_BLOCKS):
                 nc.tensor.matmul(
                     logits_ps[:, tb * P : (tb + 1) * P],
                     bias_up[jb][:, tb, :],
                     ident_f32[:],
                     is_transpose=True,
-                    start=tb == 0,
-                    stop=False,
+                    start=tb == 0 and not scores_first,
+                    stop=tb == KEY_BLOCKS - 1 and scores_first,
                 )
-            nc.tensor.matmul(
-                logits_ps[:], q_sb[h][:, jb * P : (jb + 1) * P], k_sb[h][:], start=False, stop=True
-            )
+            if not scores_first:
+                nc.tensor.matmul(
+                    logits_ps[:], q_sb[h][:, jb * P : (jb + 1) * P], k_sb[h][:], start=False, stop=True
+                )
             logit_tiles[i] = logits_ps
 
         def make_weights(i):

@@ -108,7 +108,8 @@ def tile_llamaattention_kernel(tc, base, q, k, v, attn_bias, offs, out):
             row_max = row_stats.tile([P, 1], F32, name="row_max")
             nc.vector.reduce_max(row_max[:], logits_ps[:], axis=ALONG_ROW)
             shift = row_stats.tile([P, 1], F32, name="shift")
-            nc.vector.tensor_scalar_mul(shift[:], row_max[:], -1.0 / ROOT)
+            shift_engine = nc.vector if i == len(blocks) - 1 else nc.gpsimd
+            shift_engine.tensor_scalar_mul(shift[:], row_max[:], -1.0 / ROOT)
             e_sb = weight_pool.tile([P, KEYS], BF16, name="e_sb")
             nc.scalar.activation(
                 e_sb[:], logits_ps[:], EXP, bias=shift[:], scale=1.0 / ROOT, accum_out=den[h][:, jb : jb + 1]
@@ -129,13 +130,10 @@ def tile_llamaattention_kernel(tc, base, q, k, v, attn_bias, offs, out):
                 nc.tensor.transpose(
                     spread_ps[:, jb * P : (jb + 1) * P], inv_den[:, jb : jb + 1].to_broadcast([P, P]), ident_f32[:]
                 )
-            nc.scalar.copy(inv_den_wide[h][:], spread_ps[:])
+            copy = nc.vector.tensor_copy if h == 0 else nc.scalar.copy
+            copy(inv_den_wide[h][:], spread_ps[:])
             num_ps = head_banks.tile([P, QUERIES], F32, name="num_ps")
-            if h == HEADS - 1:
-                column_groups = ((0, QUERIES - P), (QUERIES - P, QUERIES))
-            else:
-                column_groups = ((0, QUERIES),)
-            for first, last in column_groups:
+            for first, last in ((0, QUERIES - P), (QUERIES - P, QUERIES)):
                 for tb in range(KEY_BLOCKS):
                     nc.tensor.matmul(
                         num_ps[:, first:last],
@@ -144,10 +142,7 @@ def tile_llamaattention_kernel(tc, base, q, k, v, attn_bias, offs, out):
                         start=tb == 0,
                         stop=tb == KEY_BLOCKS - 1,
                     )
-            if h == 0:
-                nc.vector.tensor_copy(num_sb[h][:], num_ps[:])
-            else:
-                nc.scalar.copy(num_sb[h][:], num_ps[:])
+            copy(num_sb[h][:], num_ps[:])
 
         def place(h):
             nc.vector.tensor_tensor(windows[h][:].indirect(offsets[:]), num_sb[h][:], inv_den_wide[h][:], MULT)

@@ -108,8 +108,7 @@ def tile_llamaattention_kernel(tc, base, q, k, v, attn_bias, offs, out):
             row_max = row_stats.tile([P, 1], F32, name="row_max")
             nc.vector.reduce_max(row_max[:], logits_ps[:], axis=ALONG_ROW)
             shift = row_stats.tile([P, 1], F32, name="shift")
-            shift_engine = nc.vector if i == len(blocks) - 1 else nc.gpsimd
-            shift_engine.tensor_scalar_mul(shift[:], row_max[:], -1.0 / ROOT)
+            nc.vector.tensor_scalar_mul(shift[:], row_max[:], -1.0 / ROOT)
             e_sb = weight_pool.tile([P, KEYS], BF16, name="e_sb")
             nc.scalar.activation(
                 e_sb[:], logits_ps[:], EXP, bias=shift[:], scale=1.0 / ROOT, accum_out=den[h][:, jb : jb + 1]
@@ -133,16 +132,26 @@ def tile_llamaattention_kernel(tc, base, q, k, v, attn_bias, offs, out):
             copy = nc.vector.tensor_copy if h == 0 else nc.scalar.copy
             copy(inv_den_wide[h][:], spread_ps[:])
             num_ps = head_banks.tile([P, QUERIES], F32, name="num_ps")
-            for first, last in ((0, QUERIES - P), (QUERIES - P, QUERIES)):
+            last_num_ps = num_ps[:, QUERIES - P :]
+            if h == HEADS - 1:
+                last_bank = logit_banks.tile([P, KEYS], F32, name="last_bank", tag="logits_ps")
+                last_num_ps = last_bank[:, :P]
+            for sum_ps, first, last in (
+                (num_ps[:, : QUERIES - P], 0, QUERIES - P),
+                (last_num_ps, QUERIES - P, QUERIES),
+            ):
                 for tb in range(KEY_BLOCKS):
                     nc.tensor.matmul(
-                        num_ps[:, first:last],
+                        sum_ps,
                         v_sb[:, tb, h * P : (h + 1) * P],
                         flipped[h][:, tb, first:last],
                         start=tb == 0,
                         stop=tb == KEY_BLOCKS - 1,
                     )
-            copy(num_sb[h][:], num_ps[:])
+                if h == HEADS - 1:
+                    copy(num_sb[h][:, first:last], sum_ps)
+            if h < HEADS - 1:
+                copy(num_sb[h][:], num_ps[:])
 
         def place(h):
             nc.vector.tensor_tensor(windows[h][:].indirect(offsets[:]), num_sb[h][:], inv_den_wide[h][:], MULT)

@@ -37,14 +37,15 @@ def tile_llamaattention_kernel(tc, base, q, k, v, attn_bias, offs, out):
     ):
         q_sb = [held.tile([P, QUERIES], BF16, name=f"q_sb{h}") for h in range(HEADS)]
         k_sb = [held.tile([P, KEYS], BF16, name=f"k_sb{h}") for h in range(HEADS)]
-        for sb, src in ((q_sb[0], q), (k_sb[0], k)):
-            nc.sync.dma_start(sb[:], src[0:P, :])
         bias_by_keys = attn_bias.rearrange("(tb p) j -> p tb j", p=P)
         bias_sb = []
         for jb in range(QUERY_BLOCKS):
             bias_jb = held.tile([P, KEY_BLOCKS, P], F32, name=f"bias{jb}")
             nc.sync.dma_start(bias_jb[:], bias_by_keys[:, :, jb * P : (jb + 1) * P])
             bias_sb.append(bias_jb)
+            if jb == 0:
+                nc.sync.dma_start(q_sb[0][:], q[0:P, :])
+                nc.sync.dma_start(k_sb[0][:], k[0:P, :])
         for h in range(1, HEADS):
             nc.sync.dma_start(q_sb[h][:], q[h * P : (h + 1) * P, :])
             nc.sync.dma_start(k_sb[h][:], k[h * P : (h + 1) * P, :])
@@ -82,24 +83,18 @@ def tile_llamaattention_kernel(tc, base, q, k, v, attn_bias, offs, out):
         def make_logits(i):
             h, jb = blocks[i]
             logits_ps = logit_banks.tile([P, KEYS], F32, name="logits_ps")
-            scores_first = i < 2
-            if scores_first:
-                nc.tensor.matmul(
-                    logits_ps[:], q_sb[h][:, jb * P : (jb + 1) * P], k_sb[h][:], start=True, stop=False
-                )
             for tb in range(KEY_BLOCKS):
                 nc.tensor.matmul(
                     logits_ps[:, tb * P : (tb + 1) * P],
                     bias_up[jb][:, tb, :],
                     ident_f32[:],
                     is_transpose=True,
-                    start=tb == 0 and not scores_first,
-                    stop=tb == KEY_BLOCKS - 1 and scores_first,
+                    start=tb == 0,
+                    stop=False,
                 )
-            if not scores_first:
-                nc.tensor.matmul(
-                    logits_ps[:], q_sb[h][:, jb * P : (jb + 1) * P], k_sb[h][:], start=False, stop=True
-                )
+            nc.tensor.matmul(
+                logits_ps[:], q_sb[h][:, jb * P : (jb + 1) * P], k_sb[h][:], start=False, stop=True
+            )
             logit_tiles[i] = logits_ps
 
         def make_weights(i):

@@ -83,18 +83,24 @@ def tile_llamaattention_kernel(tc, base, q, k, v, attn_bias, offs, out):
         def make_logits(i):
             h, jb = blocks[i]
             logits_ps = logit_banks.tile([P, KEYS], F32, name="logits_ps")
+            scores_first = i > 0
+            if scores_first:
+                nc.tensor.matmul(
+                    logits_ps[:], q_sb[h][:, jb * P : (jb + 1) * P], k_sb[h][:], start=True, stop=False
+                )
             for tb in range(KEY_BLOCKS):
                 nc.tensor.matmul(
                     logits_ps[:, tb * P : (tb + 1) * P],
                     bias_up[jb][:, tb, :],
                     ident_f32[:],
                     is_transpose=True,
-                    start=tb == 0,
-                    stop=False,
+                    start=tb == 0 and not scores_first,
+                    stop=tb == KEY_BLOCKS - 1 and scores_first,
                 )
-            nc.tensor.matmul(
-                logits_ps[:], q_sb[h][:, jb * P : (jb + 1) * P], k_sb[h][:], start=False, stop=True
-            )
+            if not scores_first:
+                nc.tensor.matmul(
+                    logits_ps[:], q_sb[h][:, jb * P : (jb + 1) * P], k_sb[h][:], start=False, stop=True
+                )
             logit_tiles[i] = logits_ps
 
         def make_weights(i):

@@ -37,11 +37,13 @@ def tile_llamaattention_kernel(tc, base, q, k, v, attn_bias, offs, out):
     ):
         q_sb = [held.tile([P, QUERIES], BF16, name=f"q_sb{h}") for h in range(HEADS)]
         k_sb = [held.tile([P, KEYS], BF16, name=f"k_sb{h}") for h in range(HEADS)]
+        key_halves = (slice(0, KEY_BLOCKS // 2), slice(KEY_BLOCKS // 2, KEY_BLOCKS))
         bias_by_keys = attn_bias.rearrange("(tb p) j -> p tb j", p=P)
         bias_sb = []
         for jb in range(QUERY_BLOCKS):
             bias_jb = held.tile([P, KEY_BLOCKS, P], F32, name=f"bias{jb}")
-            nc.sync.dma_start(bias_jb[:], bias_by_keys[:, :, jb * P : (jb + 1) * P])
+            for keys in key_halves:
+                nc.sync.dma_start(bias_jb[:, keys, :], bias_by_keys[:, keys, jb * P : (jb + 1) * P])
             bias_sb.append(bias_jb)
             if jb == 0:
                 nc.sync.dma_start(q_sb[0][:], q[0:P, :])
@@ -67,10 +69,11 @@ def tile_llamaattention_kernel(tc, base, q, k, v, attn_bias, offs, out):
         bias_up = []
         for jb in range(QUERY_BLOCKS):
             bias_up_jb = held.tile([P, KEY_BLOCKS, P], F32, name=f"bias_up{jb}")
-            if jb == 0:
-                nc.vector.tensor_scalar_mul(bias_up_jb[:], bias_sb[jb][:], ROOT)
-            else:
-                nc.scalar.mul(bias_up_jb[:], bias_sb[jb][:], ROOT)
+            for keys in key_halves:
+                if jb == 0:
+                    nc.vector.tensor_scalar_mul(bias_up_jb[:, keys, :], bias_sb[jb][:, keys, :], ROOT)
+                else:
+                    nc.scalar.mul(bias_up_jb[:, keys, :], bias_sb[jb][:, keys, :], ROOT)
             bias_up.append(bias_up_jb)
 
         blocks = [(h, jb) for h in range(HEADS) for jb in range(QUERY_BLOCKS)]

@@ -120,7 +120,7 @@ def tile_llamaattention_kernel(tc, base, q, k, v, attn_bias, offs, out):
             flip_ps = flip_banks.tile([P, KEY_BLOCKS, P], BF16, name="flip_ps")
             for tb in range(KEY_BLOCKS):
                 nc.tensor.transpose(flip_ps[:, tb, :], e_sb[:, tb * P : (tb + 1) * P], ident_bf16[:])
-            if h == 0:
+            if h == 0 and jb % 2 == 1:
                 nc.vector.tensor_copy(flipped[h][:, :, jb * P : (jb + 1) * P], flip_ps[:])
             else:
                 nc.scalar.copy(flipped[h][:, :, jb * P : (jb + 1) * P], flip_ps[:])

import math

import concourse.mybir as mybir
from concourse.masks import make_identity

F32 = mybir.dt.float32
BF16 = mybir.dt.bfloat16
U16 = mybir.dt.uint16
MULT = mybir.AluOpType.mult
EXP = mybir.ActivationFunctionType.Exp
ALONG_ROW = mybir.AxisListType.X

P = 128
HEADS = 2
KEYS = 512
QUERIES = 512
TOKENS = 4096
KEY_BLOCKS = KEYS // P
QUERY_BLOCKS = QUERIES // P
ROOT = math.sqrt(P)

LOGIT_BANKS = 4
FLIP_BANKS = 2

FLOPS = 2 * HEADS * 2 * P * KEYS * QUERIES


def tile_llamaattention_kernel(tc, base, q, k, v, attn_bias, offs, out):
    nc = tc.nc
    with (
        tc.tile_pool(name="held", bufs=1) as held,
        tc.tile_pool(name="row_stats", bufs=LOGIT_BANKS) as row_stats,
        tc.tile_pool(name="weight_pool", bufs=HEADS * QUERY_BLOCKS) as weight_pool,
        tc.psum_pool(name="logit_banks", bufs=LOGIT_BANKS) as logit_banks,
        tc.psum_pool(name="flip_banks", bufs=FLIP_BANKS) as flip_banks,
        tc.psum_pool(name="head_banks", bufs=1) as head_banks,
    ):
        q_sb = [held.tile([P, QUERIES], BF16, name=f"q_sb{h}") for h in range(HEADS)]
        k_sb = [held.tile([P, KEYS], BF16, name=f"k_sb{h}") for h in range(HEADS)]
        key_halves = (slice(0, KEY_BLOCKS // 2), slice(KEY_BLOCKS // 2, KEY_BLOCKS))
        bias_by_keys = attn_bias.rearrange("(tb p) j -> p tb j", p=P)
        bias_sb = []
        for jb in range(QUERY_BLOCKS):
            bias_jb = held.tile([P, KEY_BLOCKS, P], F32, name=f"bias{jb}")
            for keys in key_halves:
                nc.sync.dma_start(bias_jb[:, keys, :], bias_by_keys[:, keys, jb * P : (jb + 1) * P])
            bias_sb.append(bias_jb)
            if jb == 0:
                nc.sync.dma_start(q_sb[0][:], q[0:P, :])
                nc.sync.dma_start(k_sb[0][:], k[0:P, :])
        for h in range(1, HEADS):
            nc.sync.dma_start(q_sb[h][:], q[h * P : (h + 1) * P, :])
            nc.sync.dma_start(k_sb[h][:], k[h * P : (h + 1) * P, :])
        v_sb = held.tile([P, KEY_BLOCKS, HEADS * P], BF16, name="v_sb")
        nc.sync.dma_start(v_sb[:], v.rearrange("(tb p) c -> p tb c", p=P))
        offsets = held.tile([P, QUERIES // 16], U16, name="offsets")
        nc.sync.dma_start(offsets[:], offs)
        windows = []
        for h in range(HEADS):
            window = held.tile([P, TOKENS], F32, name=f"window{h}")
            nc.sync.dma_start(window[:], base[h * P : (h + 1) * P, :])
            windows.append(window)

        ident_f32 = held.tile([P, P], F32, name="ident_f32")
        make_identity(nc, ident_f32[:])
        ident_bf16 = held.tile([P, P], BF16, name="ident_bf16")
        make_identity(nc, ident_bf16[:])

        bias_up = []
        for jb in range(QUERY_BLOCKS):
            bias_up_jb = held.tile([P, KEY_BLOCKS, P], F32, name=f"bias_up{jb}")
            for keys in key_halves:
                if jb == 0:
                    nc.vector.tensor_scalar_mul(bias_up_jb[:, keys, :], bias_sb[jb][:, keys, :], ROOT)
                else:
                    nc.scalar.mul(bias_up_jb[:, keys, :], bias_sb[jb][:, keys, :], ROOT)
            bias_up.append(bias_up_jb)

        blocks = [(h, jb) for h in range(HEADS) for jb in range(QUERY_BLOCKS)]
        logit_tiles = {}
        den = [held.tile([P, QUERY_BLOCKS], F32, name=f"den{h}") for h in range(HEADS)]
        flipped = [held.tile([P, KEY_BLOCKS, QUERIES], BF16, name=f"flipped{h}") for h in range(HEADS)]
        num_sb = [held.tile([P, QUERIES], F32, name=f"num_sb{h}") for h in range(HEADS)]
        inv_den_wide = [held.tile([P, QUERIES], F32, name=f"inv_den_wide{h}") for h in range(HEADS)]

        def make_logits(i):
            h, jb = blocks[i]
            logits_ps = logit_banks.tile([P, KEYS], F32, name="logits_ps")
            scores_first = i > 0
            if scores_first:
                nc.tensor.matmul(
                    logits_ps[:], q_sb[h][:, jb * P : (jb + 1) * P], k_sb[h][:], start=True, stop=False
                )
            for tb in range(KEY_BLOCKS):
                nc.tensor.matmul(
                    logits_ps[:, tb * P : (tb + 1) * P],
                    bias_up[jb][:, tb, :],
                    ident_f32[:],
                    is_transpose=True,
                    start=tb == 0 and not scores_first,
                    stop=tb == KEY_BLOCKS - 1 and scores_first,
                )
            if not scores_first:
                nc.tensor.matmul(
                    logits_ps[:], q_sb[h][:, jb * P : (jb + 1) * P], k_sb[h][:], start=False, stop=True
                )
            logit_tiles[i] = logits_ps

        def make_weights(i):
            h, jb = blocks[i]
            logits_ps = logit_tiles[i]
            row_max = row_stats.tile([P, 1], F32, name="row_max")
            nc.vector.reduce_max(row_max[:], logits_ps[:], axis=ALONG_ROW)
            shift = row_stats.tile([P, 1], F32, name="shift")
            nc.vector.tensor_scalar_mul(shift[:], row_max[:], -1.0 / ROOT)
            e_sb = weight_pool.tile([P, KEYS], BF16, name="e_sb")
            nc.scalar.activation(
                e_sb[:], logits_ps[:], EXP, bias=shift[:], scale=1.0 / ROOT, accum_out=den[h][:, jb : jb + 1]
            )
            flip_ps = flip_banks.tile([P, KEY_BLOCKS, P], BF16, name="flip_ps")
            for tb in range(KEY_BLOCKS):
                nc.tensor.transpose(flip_ps[:, tb, :], e_sb[:, tb * P : (tb + 1) * P], ident_bf16[:])
            if h == 0 and jb % 2 == 1:
                nc.vector.tensor_copy(flipped[h][:, :, jb * P : (jb + 1) * P], flip_ps[:])
            else:
                nc.scalar.copy(flipped[h][:, :, jb * P : (jb + 1) * P], flip_ps[:])

        def make_sums(h):
            inv_den = row_stats.tile([P, QUERY_BLOCKS], F32, name="inv_den")
            nc.vector.reciprocal(inv_den[:], den[h][:])
            spread_ps = head_banks.tile([P, QUERIES], F32, name="spread_ps")
            for jb in range(QUERY_BLOCKS):
                nc.tensor.transpose(
                    spread_ps[:, jb * P : (jb + 1) * P], inv_den[:, jb : jb + 1].to_broadcast([P, P]), ident_f32[:]
                )
            copy = nc.vector.tensor_copy if h == 0 else nc.scalar.copy
            copy(inv_den_wide[h][:], spread_ps[:])
            num_ps = head_banks.tile([P, QUERIES], F32, name="num_ps")
            last_num_ps = num_ps[:, QUERIES - P :]
            if h == HEADS - 1:
                last_bank = logit_banks.tile([P, KEYS], F32, name="last_bank", tag="logits_ps")
                last_num_ps = last_bank[:, :P]
            for sum_ps, first, last in (
                (num_ps[:, : QUERIES - P], 0, QUERIES - P),
                (last_num_ps, QUERIES - P, QUERIES),
            ):
                for tb in range(KEY_BLOCKS):
                    nc.tensor.matmul(
                        sum_ps,
                        v_sb[:, tb, h * P : (h + 1) * P],
                        flipped[h][:, tb, first:last],
                        start=tb == 0,
                        stop=tb == KEY_BLOCKS - 1,
                    )
                if h == HEADS - 1:
                    copy(num_sb[h][:, first:last], sum_ps)
            if h < HEADS - 1:
                copy(num_sb[h][:], num_ps[:])

        def place(h):
            nc.vector.tensor_tensor(windows[h][:].indirect(offsets[:]), num_sb[h][:], inv_den_wide[h][:], MULT)
            nc.sync.dma_start(out[h * P : (h + 1) * P, :], windows[h][:])

        for i in range(LOGIT_BANKS):
            make_logits(i)
        for i, (h, jb) in enumerate(blocks):
            make_weights(i)
            if i + LOGIT_BANKS < len(blocks):
                make_logits(i + LOGIT_BANKS)
            if jb == QUERY_BLOCKS - 1:
                if h > 0:
                    place(h - 1)
                make_sums(h)
        place(HEADS - 1)
